import numpy as np
import ml_dtypes

BF16 = ml_dtypes.bfloat16


def bf(x):
    return np.asarray(x, np.float32).astype(BF16)


def f32(x):
    return np.asarray(x, np.float32)


def f64(x):
    return np.asarray(x).astype(np.float64)


def striped(idx):
    return np.tile(idx.reshape(-1, 16).T, (8, 1))


C, S, N = 1024, 1024, 2048
T_NOW, T_SPAN = 4.0, 3.75


def setup_inputs():
    return {"alpha": f32(0.1 * np.random.standard_normal((C, S))), "event_times": f32(T_SPAN * np.random.random((1, N))), "beta": f32(1.0 + 0.1 * np.random.standard_normal((C, 1))), "base_intensity": f32(0.3 + 0.1 * np.random.standard_normal((C, 1))), "offs": striped(np.random.permutation(np.tile(np.arange(S), 2))[:N])}


def reference(alpha, event_times, beta, base_intensity, offs):
    idx = offs[:16].T.reshape(-1)
    decay = np.exp(-f64(beta) * (T_NOW - f64(event_times)))
    v = f64(base_intensity) + np.sum(f64(alpha)[:, idx] * decay, axis=1, keepdims=True)
    return np.log(1.0 + np.exp(v))

@@ -1,0 +1,86 @@
+import concourse.mybir as mybir
+
+P = 128
+C, S, N = 1024, 1024, 2048
+BLOCKS = C // P
+PIECE = S
+PIECES = N // PIECE
+T_NOW = 4.0
+
+F32 = mybir.dt.float32
+U16 = mybir.dt.uint16
+ACT = mybir.ActivationFunctionType
+ALU = mybir.AluOpType
+
+
+def tile_markedpointprocess_kernel(tc, alpha, event_times, beta, base_intensity, offs, out):
+    nc = tc.nc
+
+    alpha_blocks = alpha.rearrange("(p b) s -> b p s", b=BLOCKS)
+    beta_rows = beta.rearrange("(p b) o -> p (b o)", b=BLOCKS)
+    base_rows = base_intensity.rearrange("(p b) o -> p (b o)", b=BLOCKS)
+    out_rows = out.rearrange("(p b) o -> p (b o)", b=BLOCKS)
+
+    with (
+        tc.tile_pool(name="held", bufs=1) as held,
+        tc.tile_pool(name="decays", bufs=3) as decays,
+        tc.tile_pool(name="products", bufs=3) as products,
+    ):
+        offsets = held.tile([P, N // 16], U16, name="offsets")
+        nc.sync.dma_start(offsets[:], offs)
+
+        rate = held.tile([P, BLOCKS], F32, name="rate")
+        nc.scalar.dma_start(rate[:], beta_rows)
+        times = []
+        for h in range(PIECES):
+            times_h = held.tile([P, PIECE], F32, name=f"times{h}")
+            nc.scalar.dma_start(
+                times_h[:], event_times[:, h * PIECE : (h + 1) * PIECE].broadcast_to([P, PIECE])
+            )
+            times.append(times_h)
+        base = held.tile([P, BLOCKS], F32, name="base")
+        nc.scalar.dma_start(base[:], base_rows)
+
+        windows = []
+        for b in range(BLOCKS):
+            window = held.tile([P, S], F32, name=f"window{b}")
+            nc.sync.dma_start(window[:], alpha_blocks[b])
+            windows.append(window)
+
+        shift = held.tile([P, BLOCKS], F32, name="shift")
+        nc.vector.tensor_scalar_mul(shift[:], rate[:], -T_NOW)
+
+        partial = held.tile([P, BLOCKS * PIECES], F32, name="partial")
+
+        for b in range(BLOCKS):
+            for h in range(PIECES):
+                decay = decays.tile([P, PIECE], F32, name="decay")
+                nc.scalar.activation(
+                    decay[:], times[h][:], ACT.Exp,
+                    bias=shift[:, b : b + 1], scale=rate[:, b : b + 1],
+                )
+                product = products.tile([P, PIECE], F32, name="product")
+                piece = offsets[:, h * (PIECE // 16) : (h + 1) * (PIECE // 16)]
+                nc.vector.tensor_tensor(product[:], windows[b][:].indirect(piece), decay[:], ALU.mult)
+                k = b * PIECES + h
+                nc.scalar.activation(product[:], product[:], ACT.Copy, accum_out=partial[:, k : k + 1])
+
+        excitation = held.tile([P, BLOCKS], F32, name="excitation")
+        nc.vector.tensor_reduce(
+            excitation[:], partial[:].rearrange("p (b h) -> p b h", h=PIECES),
+            mybir.AxisListType.X, ALU.add,
+        )
+        v = held.tile([P, BLOCKS], F32, name="v")
+        nc.vector.tensor_add(v[:], excitation[:], base[:])
+
+        magnitude = held.tile([P, BLOCKS], F32, name="magnitude")
+        nc.scalar.activation(magnitude[:], v[:], ACT.Abs)
+        small = held.tile([P, BLOCKS], F32, name="small")
+        nc.scalar.activation(small[:], magnitude[:], ACT.Exp, scale=-1.0)
+        log_term = held.tile([P, BLOCKS], F32, name="log_term")
+        nc.scalar.activation(log_term[:], small[:], ACT.Ln, bias=1.0)
+        positive = held.tile([P, BLOCKS], F32, name="positive")
+        nc.vector.tensor_scalar_max(positive[:], v[:], 0.0)
+        result = held.tile([P, BLOCKS], F32, name="result")
+        nc.vector.tensor_add(result[:], positive[:], log_term[:])
+        nc.sync.dma_start(out_rows, result[:])

@@ -5,6 +5,7 @@ C, S, N = 1024, 1024, 2048
 BLOCKS = C // P
 PIECE = S
 PIECES = N // PIECE
+AHEAD = 2
 T_NOW = 4.0
 
 F32 = mybir.dt.float32
@@ -23,7 +24,7 @@ def tile_markedpointprocess_kernel(tc, alpha, event_times, beta, base_intensity,
 
     with (
         tc.tile_pool(name="held", bufs=1) as held,
-        tc.tile_pool(name="decays", bufs=3) as decays,
+        tc.tile_pool(name="decays", bufs=AHEAD + 2) as decays,
         tc.tile_pool(name="products", bufs=3) as products,
     ):
         offsets = held.tile([P, N // 16], U16, name="offsets")
@@ -50,20 +51,37 @@ def tile_markedpointprocess_kernel(tc, alpha, event_times, beta, base_intensity,
         shift = held.tile([P, BLOCKS], F32, name="shift")
         nc.vector.tensor_scalar_mul(shift[:], rate[:], -T_NOW)
 
-        partial = held.tile([P, BLOCKS * PIECES], F32, name="partial")
+        lookups = BLOCKS * PIECES
+        partial = held.tile([P, lookups], F32, name="partial")
 
-        for b in range(BLOCKS):
-            for h in range(PIECES):
-                decay = decays.tile([P, PIECE], F32, name="decay")
-                nc.scalar.activation(
-                    decay[:], times[h][:], ACT.Exp,
-                    bias=shift[:, b : b + 1], scale=rate[:, b : b + 1],
-                )
-                product = products.tile([P, PIECE], F32, name="product")
-                piece = offsets[:, h * (PIECE // 16) : (h + 1) * (PIECE // 16)]
-                nc.vector.tensor_tensor(product[:], windows[b][:].indirect(piece), decay[:], ALU.mult)
-                k = b * PIECES + h
-                nc.scalar.activation(product[:], product[:], ACT.Copy, accum_out=partial[:, k : k + 1])
+        def make_decay(k):
+            b, h = divmod(k, PIECES)
+            decay = decays.tile([P, PIECE], F32, name="decay")
+            nc.scalar.activation(
+                decay[:], times[h][:], ACT.Exp,
+                bias=shift[:, b : b + 1], scale=rate[:, b : b + 1],
+            )
+            return decay
+
+        def look_up_and_multiply(k, decay):
+            b, h = divmod(k, PIECES)
+            product = products.tile([P, PIECE], F32, name="product")
+            piece = offsets[:, h * (PIECE // 16) : (h + 1) * (PIECE // 16)]
+            nc.vector.tensor_tensor(product[:], windows[b][:].indirect(piece), decay[:], ALU.mult)
+            return product
+
+        def add_up(k, product):
+            nc.scalar.activation(product[:], product[:], ACT.Copy, accum_out=partial[:, k : k + 1])
+
+        decay_of = {k: make_decay(k) for k in range(AHEAD)}
+        product_of = {}
+        for k in range(lookups):
+            product_of[k] = look_up_and_multiply(k, decay_of[k])
+            if k + AHEAD < lookups:
+                decay_of[k + AHEAD] = make_decay(k + AHEAD)
+            if k >= 1:
+                add_up(k - 1, product_of[k - 1])
+        add_up(lookups - 1, product_of[lookups - 1])
 
         excitation = held.tile([P, BLOCKS], F32, name="excitation")
         nc.vector.tensor_reduce(

@@ -1,11 +1,15 @@
 import concourse.mybir as mybir
+from concourse.masks import make_identity
 
 P = 128
 C, S, N = 1024, 1024, 2048
 BLOCKS = C // P
 PIECE = S
 PIECES = N // PIECE
+LOOKUPS = BLOCKS * PIECES
+BANK = 512
 AHEAD = 2
+BEHIND = 3
 T_NOW = 4.0
 
 F32 = mybir.dt.float32
@@ -25,34 +29,38 @@ def tile_markedpointprocess_kernel(tc, alpha, event_times, beta, base_intensity,
     with (
         tc.tile_pool(name="held", bufs=1) as held,
         tc.tile_pool(name="decays", bufs=AHEAD + 2) as decays,
-        tc.tile_pool(name="products", bufs=3) as products,
+        tc.tile_pool(name="products", bufs=4) as products,
+        tc.psum_pool(name="banks", bufs=2) as banks,
     ):
+        zero = held.tile([P, 1], F32, name="zero")
+        nc.vector.memset(zero[:], 0.0)
+        one = held.tile([P, 1], F32, name="one")
+        nc.scalar.activation(one[:], zero[:], ACT.Exp)
+
         offsets = held.tile([P, N // 16], U16, name="offsets")
-        nc.sync.dma_start(offsets[:], offs)
-
         rate = held.tile([P, BLOCKS], F32, name="rate")
-        nc.scalar.dma_start(rate[:], beta_rows)
-        times = []
-        for h in range(PIECES):
-            times_h = held.tile([P, PIECE], F32, name=f"times{h}")
-            nc.scalar.dma_start(
-                times_h[:], event_times[:, h * PIECE : (h + 1) * PIECE].broadcast_to([P, PIECE])
-            )
-            times.append(times_h)
         base = held.tile([P, BLOCKS], F32, name="base")
-        nc.scalar.dma_start(base[:], base_rows)
+        times = [held.tile([P, PIECE], F32, name=f"times{h}") for h in range(PIECES)]
+        windows = [held.tile([P, S], F32, name=f"window{b}") for b in range(BLOCKS)]
 
-        windows = []
+        nc.sync.dma_start(offsets[:], offs)
+        nc.sync.dma_start(rate[:], beta_rows)
         for b in range(BLOCKS):
-            window = held.tile([P, S], F32, name=f"window{b}")
-            nc.sync.dma_start(window[:], alpha_blocks[b])
-            windows.append(window)
+            if b < PIECES:
+                piece_of_times = event_times[:, b * PIECE : (b + 1) * PIECE]
+                nc.sync.dma_start(times[b][:], piece_of_times.broadcast_to([P, PIECE]))
+            nc.sync.dma_start(windows[b][:], alpha_blocks[b])
+        nc.sync.dma_start(base[:], base_rows)
+
+        identity = held.tile([P, P], F32, name="identity")
+        make_identity(nc, identity[:])
 
         shift = held.tile([P, BLOCKS], F32, name="shift")
         nc.vector.tensor_scalar_mul(shift[:], rate[:], -T_NOW)
 
-        lookups = BLOCKS * PIECES
-        partial = held.tile([P, lookups], F32, name="partial")
+        partial = held.tile([P, LOOKUPS], F32, name="partial")
+        nc.vector.memset(partial[:], 0.0)
+        discard = held.tile([P, BANK], F32, name="discard")
 
         def make_decay(k):
             b, h = divmod(k, PIECES)
@@ -70,18 +78,37 @@ def tile_markedpointprocess_kernel(tc, alpha, event_times, beta, base_intensity,
             nc.vector.tensor_tensor(product[:], windows[b][:].indirect(piece), decay[:], ALU.mult)
             return product
 
-        def add_up(k, product):
-            nc.scalar.activation(product[:], product[:], ACT.Copy, accum_out=partial[:, k : k + 1])
+        def fold(k, product, bank):
+            h = k % PIECES
+            for q in range(PIECE // BANK):
+                nc.tensor.matmul(
+                    bank[:], identity[:], product[:, q * BANK : (q + 1) * BANK],
+                    start=(h == 0 and q == 0),
+                    stop=(h == PIECES - 1 and q == PIECE // BANK - 1),
+                )
+
+        def add_up(k, values, copy_to):
+            nc.scalar.activation(copy_to, values, ACT.Copy, accum_out=partial[:, k : k + 1])
 
         decay_of = {k: make_decay(k) for k in range(AHEAD)}
         product_of = {}
-        for k in range(lookups):
-            product_of[k] = look_up_and_multiply(k, decay_of[k])
-            if k + AHEAD < lookups:
+        bank_of = {}
+        for k in range(LOOKUPS + BEHIND):
+            if k < LOOKUPS:
+                product_of[k] = look_up_and_multiply(k, decay_of[k])
+                b = k // PIECES
+                if b % 2 == 0:
+                    if k % PIECES == 0:
+                        bank_of[b] = banks.tile([P, BANK], F32, name="bank")
+                    fold(k, product_of[k], bank_of[b])
+            if k + AHEAD < LOOKUPS:
                 decay_of[k + AHEAD] = make_decay(k + AHEAD)
-            if k >= 1:
-                add_up(k - 1, product_of[k - 1])
-        add_up(lookups - 1, product_of[lookups - 1])
+            folded = k - BEHIND
+            if folded >= 0 and folded % (2 * PIECES) == PIECES - 1:
+                add_up(folded, bank_of[folded // PIECES][:], discard[:])
+            done = k - 1
+            if 0 <= done < LOOKUPS and (done // PIECES) % 2 == 1:
+                add_up(done, product_of[done][:], product_of[done][:])
 
         excitation = held.tile([P, BLOCKS], F32, name="excitation")
         nc.vector.tensor_reduce(
@@ -96,7 +123,7 @@ def tile_markedpointprocess_kernel(tc, alpha, event_times, beta, base_intensity,
         small = held.tile([P, BLOCKS], F32, name="small")
         nc.scalar.activation(small[:], magnitude[:], ACT.Exp, scale=-1.0)
         log_term = held.tile([P, BLOCKS], F32, name="log_term")
-        nc.scalar.activation(log_term[:], small[:], ACT.Ln, bias=1.0)
+        nc.scalar.activation(log_term[:], small[:], ACT.Ln, bias=one[:])
         positive = held.tile([P, BLOCKS], F32, name="positive")
         nc.vector.tensor_scalar_max(positive[:], v[:], 0.0)
         result = held.tile([P, BLOCKS], F32, name="result")

@@ -32,25 +32,25 @@ def tile_markedpointprocess_kernel(tc, alpha, event_times, beta, base_intensity,
         tc.tile_pool(name="products", bufs=4) as products,
         tc.psum_pool(name="banks", bufs=2) as banks,
     ):
-        zero = held.tile([P, 1], F32, name="zero")
-        nc.vector.memset(zero[:], 0.0)
-        one = held.tile([P, 1], F32, name="one")
-        nc.scalar.activation(one[:], zero[:], ACT.Exp)
-
         offsets = held.tile([P, N // 16], U16, name="offsets")
         rate = held.tile([P, BLOCKS], F32, name="rate")
         base = held.tile([P, BLOCKS], F32, name="base")
         times = [held.tile([P, PIECE], F32, name=f"times{h}") for h in range(PIECES)]
         windows = [held.tile([P, S], F32, name=f"window{b}") for b in range(BLOCKS)]
 
+        nc.scalar.dma_start(rate[:], beta_rows)
+        for h in range(PIECES):
+            piece_of_times = event_times[:, h * PIECE : (h + 1) * PIECE]
+            nc.scalar.dma_start(times[h][:], piece_of_times.broadcast_to([P, PIECE]))
+        nc.scalar.dma_start(base[:], base_rows)
         nc.sync.dma_start(offsets[:], offs)
-        nc.sync.dma_start(rate[:], beta_rows)
         for b in range(BLOCKS):
-            if b < PIECES:
-                piece_of_times = event_times[:, b * PIECE : (b + 1) * PIECE]
-                nc.sync.dma_start(times[b][:], piece_of_times.broadcast_to([P, PIECE]))
             nc.sync.dma_start(windows[b][:], alpha_blocks[b])
-        nc.sync.dma_start(base[:], base_rows)
+
+        zero = held.tile([P, 1], F32, name="zero")
+        nc.vector.memset(zero[:], 0.0)
+        one = held.tile([P, 1], F32, name="one")
+        nc.scalar.activation(one[:], zero[:], ACT.Exp)
 
         identity = held.tile([P, P], F32, name="identity")
         make_identity(nc, identity[:])

@@ -1,5 +1,4 @@
 import concourse.mybir as mybir
-from concourse.masks import make_identity
 
 P = 128
 C, S, N = 1024, 1024, 2048
@@ -7,9 +6,7 @@ BLOCKS = C // P
 PIECE = S
 PIECES = N // PIECE
 LOOKUPS = BLOCKS * PIECES
-BANK = 512
 AHEAD = 2
-BEHIND = 3
 T_NOW = 4.0
 
 F32 = mybir.dt.float32
@@ -29,8 +26,7 @@ def tile_markedpointprocess_kernel(tc, alpha, event_times, beta, base_intensity,
     with (
         tc.tile_pool(name="held", bufs=1) as held,
         tc.tile_pool(name="decays", bufs=AHEAD + 2) as decays,
-        tc.tile_pool(name="products", bufs=4) as products,
-        tc.psum_pool(name="banks", bufs=2) as banks,
+        tc.tile_pool(name="products", bufs=3) as products,
     ):
         offsets = held.tile([P, N // 16], U16, name="offsets")
         rate = held.tile([P, BLOCKS], F32, name="rate")
@@ -52,15 +48,10 @@ def tile_markedpointprocess_kernel(tc, alpha, event_times, beta, base_intensity,
         one = held.tile([P, 1], F32, name="one")
         nc.scalar.activation(one[:], zero[:], ACT.Exp)
 
-        identity = held.tile([P, P], F32, name="identity")
-        make_identity(nc, identity[:])
-
         shift = held.tile([P, BLOCKS], F32, name="shift")
         nc.vector.tensor_scalar_mul(shift[:], rate[:], -T_NOW)
 
         partial = held.tile([P, LOOKUPS], F32, name="partial")
-        nc.vector.memset(partial[:], 0.0)
-        discard = held.tile([P, BANK], F32, name="discard")
 
         def make_decay(k):
             b, h = divmod(k, PIECES)
@@ -78,37 +69,18 @@ def tile_markedpointprocess_kernel(tc, alpha, event_times, beta, base_intensity,
             nc.vector.tensor_tensor(product[:], windows[b][:].indirect(piece), decay[:], ALU.mult)
             return product
 
-        def fold(k, product, bank):
-            h = k % PIECES
-            for q in range(PIECE // BANK):
-                nc.tensor.matmul(
-                    bank[:], identity[:], product[:, q * BANK : (q + 1) * BANK],
-                    start=(h == 0 and q == 0),
-                    stop=(h == PIECES - 1 and q == PIECE // BANK - 1),
-                )
-
-        def add_up(k, values, copy_to):
-            nc.scalar.activation(copy_to, values, ACT.Copy, accum_out=partial[:, k : k + 1])
+        def add_up(k, product):
+            nc.scalar.activation(product[:], product[:], ACT.Copy, accum_out=partial[:, k : k + 1])
 
         decay_of = {k: make_decay(k) for k in range(AHEAD)}
         product_of = {}
-        bank_of = {}
-        for k in range(LOOKUPS + BEHIND):
-            if k < LOOKUPS:
-                product_of[k] = look_up_and_multiply(k, decay_of[k])
-                b = k // PIECES
-                if b % 2 == 0:
-                    if k % PIECES == 0:
-                        bank_of[b] = banks.tile([P, BANK], F32, name="bank")
-                    fold(k, product_of[k], bank_of[b])
+        for k in range(LOOKUPS):
+            product_of[k] = look_up_and_multiply(k, decay_of[k])
             if k + AHEAD < LOOKUPS:
                 decay_of[k + AHEAD] = make_decay(k + AHEAD)
-            folded = k - BEHIND
-            if folded >= 0 and folded % (2 * PIECES) == PIECES - 1:
-                add_up(folded, bank_of[folded // PIECES][:], discard[:])
-            done = k - 1
-            if 0 <= done < LOOKUPS and (done // PIECES) % 2 == 1:
-                add_up(done, product_of[done][:], product_of[done][:])
+            if k >= 1:
+                add_up(k - 1, product_of[k - 1])
+        add_up(LOOKUPS - 1, product_of[LOOKUPS - 1])
 
         excitation = held.tile([P, BLOCKS], F32, name="excitation")
         nc.vector.tensor_reduce(

@@ -4,15 +4,26 @@ P = 128
 C, S, N = 1024, 1024, 2048
 BLOCKS = C // P
 PIECE = S
-PIECES = N // PIECE
-LOOKUPS = BLOCKS * PIECES
-AHEAD = 2
+FIRST_CUTS = (256, 256, 512, 512, 512)
+SLOTS = len(FIRST_CUTS)
+AHEAD = 3
+BEHIND = 2
 T_NOW = 4.0
 
 F32 = mybir.dt.float32
 U16 = mybir.dt.uint16
 ACT = mybir.ActivationFunctionType
 ALU = mybir.AluOpType
+
+
+def look_ups():
+    plan = []
+    for b in range(BLOCKS):
+        first = 0
+        for slot, width in enumerate(FIRST_CUTS if b == 0 else (PIECE, PIECE)):
+            plan.append((b, slot, first, width))
+            first += width
+    return plan
 
 
 def tile_markedpointprocess_kernel(tc, alpha, event_times, beta, base_intensity, offs, out):
@@ -26,65 +37,80 @@ def tile_markedpointprocess_kernel(tc, alpha, event_times, beta, base_intensity,
     with (
         tc.tile_pool(name="held", bufs=1) as held,
         tc.tile_pool(name="decays", bufs=AHEAD + 2) as decays,
-        tc.tile_pool(name="products", bufs=3) as products,
+        tc.tile_pool(name="products", bufs=BEHIND + 2) as products,
     ):
         offsets = held.tile([P, N // 16], U16, name="offsets")
         rate = held.tile([P, BLOCKS], F32, name="rate")
         base = held.tile([P, BLOCKS], F32, name="base")
-        times = [held.tile([P, PIECE], F32, name=f"times{h}") for h in range(PIECES)]
+        times = held.tile([P, N], F32, name="times")
         windows = [held.tile([P, S], F32, name=f"window{b}") for b in range(BLOCKS)]
 
+        plan = look_ups()
+
+        def load_times(queue, first, width):
+            some_times = event_times[:, first : first + width]
+            queue.dma_start(times[:, first : first + width], some_times.broadcast_to([P, width]))
+
         nc.scalar.dma_start(rate[:], beta_rows)
-        for h in range(PIECES):
-            piece_of_times = event_times[:, h * PIECE : (h + 1) * PIECE]
-            nc.scalar.dma_start(times[h][:], piece_of_times.broadcast_to([P, PIECE]))
-        nc.scalar.dma_start(base[:], base_rows)
+        load_times(nc.scalar, 0, FIRST_CUTS[0])
         nc.sync.dma_start(offsets[:], offs)
-        for b in range(BLOCKS):
+        nc.sync.dma_start(windows[0][:], alpha_blocks[0])
+        for b, slot, first, width in plan[1:SLOTS]:
+            load_times(nc.sync, first, width)
+        for b in range(1, BLOCKS):
             nc.sync.dma_start(windows[b][:], alpha_blocks[b])
+        nc.sync.dma_start(base[:], base_rows)
 
         zero = held.tile([P, 1], F32, name="zero")
-        nc.vector.memset(zero[:], 0.0)
+        nc.gpsimd.memset(zero[:], 0.0)
         one = held.tile([P, 1], F32, name="one")
         nc.scalar.activation(one[:], zero[:], ACT.Exp)
 
         shift = held.tile([P, BLOCKS], F32, name="shift")
-        nc.vector.tensor_scalar_mul(shift[:], rate[:], -T_NOW)
+        nc.scalar.mul(shift[:], rate[:], -T_NOW)
 
-        partial = held.tile([P, LOOKUPS], F32, name="partial")
+        partial = held.tile([P, BLOCKS * SLOTS], F32, name="partial")
+        nc.gpsimd.memset(partial[:], 0.0)
 
         def make_decay(k):
-            b, h = divmod(k, PIECES)
+            b, slot, first, width = plan[k]
             decay = decays.tile([P, PIECE], F32, name="decay")
             nc.scalar.activation(
-                decay[:], times[h][:], ACT.Exp,
+                decay[:, :width], times[:, first : first + width], ACT.Exp,
                 bias=shift[:, b : b + 1], scale=rate[:, b : b + 1],
             )
             return decay
 
         def look_up_and_multiply(k, decay):
-            b, h = divmod(k, PIECES)
+            b, slot, first, width = plan[k]
             product = products.tile([P, PIECE], F32, name="product")
-            piece = offsets[:, h * (PIECE // 16) : (h + 1) * (PIECE // 16)]
-            nc.vector.tensor_tensor(product[:], windows[b][:].indirect(piece), decay[:], ALU.mult)
+            piece = offsets[:, first // 16 : (first + width) // 16]
+            nc.vector.tensor_tensor(
+                product[:, :width], windows[b][:].indirect(piece), decay[:, :width], ALU.mult
+            )
             return product
 
         def add_up(k, product):
-            nc.scalar.activation(product[:], product[:], ACT.Copy, accum_out=partial[:, k : k + 1])
+            b, slot, first, width = plan[k]
+            nc.scalar.activation(
+                product[:, :width], product[:, :width], ACT.Copy,
+                accum_out=partial[:, b * SLOTS + slot : b * SLOTS + slot + 1],
+            )
 
         decay_of = {k: make_decay(k) for k in range(AHEAD)}
         product_of = {}
-        for k in range(LOOKUPS):
+        for k in range(len(plan)):
             product_of[k] = look_up_and_multiply(k, decay_of[k])
-            if k + AHEAD < LOOKUPS:
+            if k + AHEAD < len(plan):
                 decay_of[k + AHEAD] = make_decay(k + AHEAD)
-            if k >= 1:
-                add_up(k - 1, product_of[k - 1])
-        add_up(LOOKUPS - 1, product_of[LOOKUPS - 1])
+            if k >= BEHIND:
+                add_up(k - BEHIND, product_of[k - BEHIND])
+        for k in range(len(plan) - BEHIND, len(plan)):
+            add_up(k, product_of[k])
 
         excitation = held.tile([P, BLOCKS], F32, name="excitation")
         nc.vector.tensor_reduce(
-            excitation[:], partial[:].rearrange("p (b h) -> p b h", h=PIECES),
+            excitation[:], partial[:].rearrange("p (b h) -> p b h", h=SLOTS),
             mybir.AxisListType.X, ALU.add,
         )
         v = held.tile([P, BLOCKS], F32, name="v")

@@ -4,8 +4,8 @@ P = 128
 C, S, N = 1024, 1024, 2048
 BLOCKS = C // P
 PIECE = S
-FIRST_CUTS = (256, 256, 512, 512, 512)
-SLOTS = len(FIRST_CUTS)
+BANK = 512
+SLOTS = N // BANK
 AHEAD = 3
 BEHIND = 2
 T_NOW = 4.0
@@ -19,10 +19,9 @@ ALU = mybir.AluOpType
 def look_ups():
     plan = []
     for b in range(BLOCKS):
-        first = 0
-        for slot, width in enumerate(FIRST_CUTS if b == 0 else (PIECE, PIECE)):
-            plan.append((b, slot, first, width))
-            first += width
+        width = BANK if b == 0 else PIECE
+        for slot in range(N // width):
+            plan.append((b, slot, slot * width, width))
     return plan
 
 
@@ -38,28 +37,28 @@ def tile_markedpointprocess_kernel(tc, alpha, event_times, beta, base_intensity,
         tc.tile_pool(name="held", bufs=1) as held,
         tc.tile_pool(name="decays", bufs=AHEAD + 2) as decays,
         tc.tile_pool(name="products", bufs=BEHIND + 2) as products,
+        tc.psum_pool(name="banks", bufs=1) as banks,
     ):
         offsets = held.tile([P, N // 16], U16, name="offsets")
         rate = held.tile([P, BLOCKS], F32, name="rate")
         base = held.tile([P, BLOCKS], F32, name="base")
-        times = held.tile([P, N], F32, name="times")
+        time_row = held.tile([1, N], F32, name="time_row")
         windows = [held.tile([P, S], F32, name=f"window{b}") for b in range(BLOCKS)]
 
         plan = look_ups()
 
-        def load_times(queue, first, width):
-            some_times = event_times[:, first : first + width]
-            queue.dma_start(times[:, first : first + width], some_times.broadcast_to([P, width]))
-
+        nc.scalar.dma_start(time_row[:], event_times)
         nc.scalar.dma_start(rate[:], beta_rows)
-        load_times(nc.scalar, 0, FIRST_CUTS[0])
         nc.sync.dma_start(offsets[:], offs)
-        nc.sync.dma_start(windows[0][:], alpha_blocks[0])
-        for b, slot, first, width in plan[1:SLOTS]:
-            load_times(nc.sync, first, width)
-        for b in range(1, BLOCKS):
+        for b in range(BLOCKS):
             nc.sync.dma_start(windows[b][:], alpha_blocks[b])
         nc.sync.dma_start(base[:], base_rows)
+
+        ones = held.tile([1, P], F32, name="ones")
+        nc.gpsimd.memset(ones[:], 1.0)
+        times = [banks.tile([P, BANK], F32, name=f"times{i}") for i in range(N // BANK)]
+        for i in range(N // BANK):
+            nc.tensor.matmul(times[i][:], ones[:], time_row[:, i * BANK : (i + 1) * BANK])
 
         zero = held.tile([P, 1], F32, name="zero")
         nc.gpsimd.memset(zero[:], 0.0)
@@ -75,10 +74,11 @@ def tile_markedpointprocess_kernel(tc, alpha, event_times, beta, base_intensity,
         def make_decay(k):
             b, slot, first, width = plan[k]
             decay = decays.tile([P, PIECE], F32, name="decay")
-            nc.scalar.activation(
-                decay[:, :width], times[:, first : first + width], ACT.Exp,
-                bias=shift[:, b : b + 1], scale=rate[:, b : b + 1],
-            )
+            for i in range(width // BANK):
+                nc.scalar.activation(
+                    decay[:, i * BANK : (i + 1) * BANK], times[first // BANK + i][:], ACT.Exp,
+                    bias=shift[:, b : b + 1], scale=rate[:, b : b + 1],
+                )
             return decay
 
         def look_up_and_multiply(k, decay):

@@ -1,4 +1,5 @@
 import concourse.mybir as mybir
+from concourse.masks import make_identity
 
 P = 128
 C, S, N = 1024, 1024, 2048
@@ -42,23 +43,28 @@ def tile_markedpointprocess_kernel(tc, alpha, event_times, beta, base_intensity,
         offsets = held.tile([P, N // 16], U16, name="offsets")
         rate = held.tile([P, BLOCKS], F32, name="rate")
         base = held.tile([P, BLOCKS], F32, name="base")
-        time_row = held.tile([1, N], F32, name="time_row")
+        time_columns = held.tile([P, N // P], F32, name="time_columns")
         windows = [held.tile([P, S], F32, name=f"window{b}") for b in range(BLOCKS)]
 
         plan = look_ups()
 
-        nc.scalar.dma_start(time_row[:], event_times)
+        nc.scalar.dma_start(time_columns[:], event_times.rearrange("o (i p) -> p (o i)", p=P))
         nc.scalar.dma_start(rate[:], beta_rows)
         nc.sync.dma_start(offsets[:], offs)
         for b in range(BLOCKS):
             nc.sync.dma_start(windows[b][:], alpha_blocks[b])
         nc.sync.dma_start(base[:], base_rows)
 
-        ones = held.tile([1, P], F32, name="ones")
-        nc.gpsimd.memset(ones[:], 1.0)
+        identity = held.tile([P, P], F32, name="identity")
+        make_identity(nc, identity[:])
         times = [banks.tile([P, BANK], F32, name=f"times{i}") for i in range(N // BANK)]
-        for i in range(N // BANK):
-            nc.tensor.matmul(times[i][:], ones[:], time_row[:, i * BANK : (i + 1) * BANK])
+        for i in range(N // P):
+            bank, place = divmod(i * P, BANK)
+            nc.tensor.transpose(
+                times[bank][:, place : place + P],
+                time_columns[:, i : i + 1].to_broadcast([P, P]),
+                identity[:],
+            )
 
         zero = held.tile([P, 1], F32, name="zero")
         nc.gpsimd.memset(zero[:], 0.0)

@@ -43,12 +43,14 @@ def tile_markedpointprocess_kernel(tc, alpha, event_times, beta, base_intensity,
         offsets = held.tile([P, N // 16], U16, name="offsets")
         rate = held.tile([P, BLOCKS], F32, name="rate")
         base = held.tile([P, BLOCKS], F32, name="base")
+        time_rows = held.tile([P, P], F32, name="time_rows")
         time_columns = held.tile([P, N // P], F32, name="time_columns")
         windows = [held.tile([P, S], F32, name=f"window{b}") for b in range(BLOCKS)]
 
         plan = look_ups()
 
-        nc.scalar.dma_start(time_columns[:], event_times.rearrange("o (i p) -> p (o i)", p=P))
+        nc.gpsimd.memset(time_rows[:], 0.0)
+        nc.sync.dma_start(time_rows[: N // P, :], event_times.rearrange("o (i p) -> (o i) p", p=P))
         nc.scalar.dma_start(rate[:], beta_rows)
         nc.sync.dma_start(offsets[:], offs)
         for b in range(BLOCKS):
@@ -57,6 +59,10 @@ def tile_markedpointprocess_kernel(tc, alpha, event_times, beta, base_intensity,
 
         identity = held.tile([P, P], F32, name="identity")
         make_identity(nc, identity[:])
+        turned = banks.tile([P, P], F32, name="turned")
+        nc.tensor.transpose(turned[:], time_rows[:], identity[:])
+        nc.vector.tensor_copy(time_columns[:], turned[:, : N // P])
+
         times = [banks.tile([P, BANK], F32, name=f"times{i}") for i in range(N // BANK)]
         for i in range(N // P):
             bank, place = divmod(i * P, BANK)

@@ -6,7 +6,8 @@ C, S, N = 1024, 1024, 2048
 BLOCKS = C // P
 PIECE = S
 BANK = 512
-SLOTS = N // BANK
+RAMP = (P, P, 2 * P, BANK, BANK, BANK)
+SLOTS = len(RAMP)
 AHEAD = 3
 BEHIND = 2
 T_NOW = 4.0
@@ -20,9 +21,10 @@ ALU = mybir.AluOpType
 def look_ups():
     plan = []
     for b in range(BLOCKS):
-        width = BANK if b == 0 else PIECE
-        for slot in range(N // width):
-            plan.append((b, slot, slot * width, width))
+        first = 0
+        for slot, width in enumerate(RAMP if b == 0 else (PIECE, PIECE)):
+            plan.append((b, slot, first, width))
+            first += width
     return plan
 
 
@@ -37,7 +39,7 @@ def tile_markedpointprocess_kernel(tc, alpha, event_times, beta, base_intensity,
     with (
         tc.tile_pool(name="held", bufs=1) as held,
         tc.tile_pool(name="decays", bufs=AHEAD + 2) as decays,
-        tc.tile_pool(name="products", bufs=BEHIND + 2) as products,
+        tc.tile_pool(name="products", bufs=BEHIND + SLOTS) as products,
         tc.psum_pool(name="banks", bufs=1) as banks,
     ):
         offsets = held.tile([P, N // 16], U16, name="offsets")
@@ -63,14 +65,15 @@ def tile_markedpointprocess_kernel(tc, alpha, event_times, beta, base_intensity,
         nc.tensor.transpose(turned[:], time_rows[:], identity[:])
         nc.vector.tensor_copy(time_columns[:], turned[:, : N // P])
 
-        times = [banks.tile([P, BANK], F32, name=f"times{i}") for i in range(N // BANK)]
-        for i in range(N // P):
-            bank, place = divmod(i * P, BANK)
-            nc.tensor.transpose(
-                times[bank][:, place : place + P],
-                time_columns[:, i : i + 1].to_broadcast([P, P]),
-                identity[:],
-            )
+        times = [banks.tile([P, BANK], F32, name=f"times{slot}") for slot in range(SLOTS)]
+        for b, slot, first, width in plan[:SLOTS]:
+            for place in range(0, width, P):
+                i = (first + place) // P
+                nc.tensor.transpose(
+                    times[slot][:, place : place + P],
+                    time_columns[:, i : i + 1].to_broadcast([P, P]),
+                    identity[:],
+                )
 
         zero = held.tile([P, 1], F32, name="zero")
         nc.gpsimd.memset(zero[:], 0.0)
@@ -86,11 +89,15 @@ def tile_markedpointprocess_kernel(tc, alpha, event_times, beta, base_intensity,
         def make_decay(k):
             b, slot, first, width = plan[k]
             decay = decays.tile([P, PIECE], F32, name="decay")
-            for i in range(width // BANK):
-                nc.scalar.activation(
-                    decay[:, i * BANK : (i + 1) * BANK], times[first // BANK + i][:], ACT.Exp,
-                    bias=shift[:, b : b + 1], scale=rate[:, b : b + 1],
-                )
+            for block0, bank, bank_first, bank_width in plan[:SLOTS]:
+                lo = max(first, bank_first)
+                hi = min(first + width, bank_first + bank_width)
+                if lo < hi:
+                    nc.scalar.activation(
+                        decay[:, lo - first : hi - first],
+                        times[bank][:, lo - bank_first : hi - bank_first], ACT.Exp,
+                        bias=shift[:, b : b + 1], scale=rate[:, b : b + 1],
+                    )
             return decay
 
         def look_up_and_multiply(k, decay):

@@ -19,10 +19,13 @@ ALU = mybir.AluOpType
 
 
 def look_ups():
+    widths_of = {b: (PIECE, PIECE) for b in range(BLOCKS)}
+    widths_of[0] = RAMP
+    widths_of[BLOCKS - 1] = tuple(reversed(RAMP))
     plan = []
     for b in range(BLOCKS):
         first = 0
-        for slot, width in enumerate(RAMP if b == 0 else (PIECE, PIECE)):
+        for slot, width in enumerate(widths_of[b]):
             plan.append((b, slot, first, width))
             first += width
     return plan
@@ -47,12 +50,14 @@ def tile_markedpointprocess_kernel(tc, alpha, event_times, beta, base_intensity,
         base = held.tile([P, BLOCKS], F32, name="base")
         time_rows = held.tile([P, P], F32, name="time_rows")
         time_columns = held.tile([P, N // P], F32, name="time_columns")
+        first_column = held.tile([P, 1], F32, name="first_column")
         windows = [held.tile([P, S], F32, name=f"window{b}") for b in range(BLOCKS)]
 
         plan = look_ups()
 
         nc.gpsimd.memset(time_rows[:], 0.0)
         nc.sync.dma_start(time_rows[: N // P, :], event_times.rearrange("o (i p) -> (o i) p", p=P))
+        nc.scalar.dma_start(first_column[:], event_times[:, :P].rearrange("o p -> p o"))
         nc.scalar.dma_start(rate[:], beta_rows)
         nc.sync.dma_start(offsets[:], offs)
         for b in range(BLOCKS):
@@ -61,19 +66,21 @@ def tile_markedpointprocess_kernel(tc, alpha, event_times, beta, base_intensity,
 
         identity = held.tile([P, P], F32, name="identity")
         make_identity(nc, identity[:])
+        times = [banks.tile([P, BANK], F32, name=f"times{slot}") for slot in range(SLOTS)]
+
+        def spread(column, slot, place):
+            nc.tensor.transpose(
+                times[slot][:, place : place + P], column.to_broadcast([P, P]), identity[:]
+            )
+
+        spread(first_column[:], 0, 0)
         turned = banks.tile([P, P], F32, name="turned")
         nc.tensor.transpose(turned[:], time_rows[:], identity[:])
         nc.vector.tensor_copy(time_columns[:], turned[:, : N // P])
-
-        times = [banks.tile([P, BANK], F32, name=f"times{slot}") for slot in range(SLOTS)]
-        for b, slot, first, width in plan[:SLOTS]:
+        for b, slot, first, width in plan[1:SLOTS]:
             for place in range(0, width, P):
                 i = (first + place) // P
-                nc.tensor.transpose(
-                    times[slot][:, place : place + P],
-                    time_columns[:, i : i + 1].to_broadcast([P, P]),
-                    identity[:],
-                )
+                spread(time_columns[:, i : i + 1], slot, place)
 
         zero = held.tile([P, 1], F32, name="zero")
         nc.gpsimd.memset(zero[:], 0.0)

@@ -8,6 +8,7 @@ PIECE = S
 BANK = 512
 RAMP = (P, P, 2 * P, BANK, BANK, BANK)
 SLOTS = len(RAMP)
+PARTS = SLOTS + 1
 AHEAD = 3
 BEHIND = 2
 T_NOW = 4.0
@@ -57,12 +58,12 @@ def tile_markedpointprocess_kernel(tc, alpha, event_times, beta, base_intensity,
 
         nc.gpsimd.memset(time_rows[:], 0.0)
         nc.sync.dma_start(time_rows[: N // P, :], event_times.rearrange("o (i p) -> (o i) p", p=P))
+        nc.sync.dma_start(base[:], base_rows)
         nc.scalar.dma_start(first_column[:], event_times[:, :P].rearrange("o p -> p o"))
         nc.scalar.dma_start(rate[:], beta_rows)
         nc.sync.dma_start(offsets[:], offs)
         for b in range(BLOCKS):
             nc.sync.dma_start(windows[b][:], alpha_blocks[b])
-        nc.sync.dma_start(base[:], base_rows)
 
         identity = held.tile([P, P], F32, name="identity")
         make_identity(nc, identity[:])
@@ -90,8 +91,10 @@ def tile_markedpointprocess_kernel(tc, alpha, event_times, beta, base_intensity,
         shift = held.tile([P, BLOCKS], F32, name="shift")
         nc.scalar.mul(shift[:], rate[:], -T_NOW)
 
-        partial = held.tile([P, BLOCKS * SLOTS], F32, name="partial")
+        partial = held.tile([P, BLOCKS * PARTS], F32, name="partial")
+        parts = partial[:].rearrange("p (b h) -> p b h", h=PARTS)
         nc.gpsimd.memset(partial[:], 0.0)
+        nc.vector.tensor_copy(parts[:, :, SLOTS : SLOTS + 1], base[:].unsqueeze(2))
 
         def make_decay(k):
             b, slot, first, width = plan[k]
@@ -120,7 +123,7 @@ def tile_markedpointprocess_kernel(tc, alpha, event_times, beta, base_intensity,
             b, slot, first, width = plan[k]
             nc.scalar.activation(
                 product[:, :width], product[:, :width], ACT.Copy,
-                accum_out=partial[:, b * SLOTS + slot : b * SLOTS + slot + 1],
+                accum_out=partial[:, b * PARTS + slot : b * PARTS + slot + 1],
             )
 
         decay_of = {k: make_decay(k) for k in range(AHEAD)}
@@ -134,13 +137,8 @@ def tile_markedpointprocess_kernel(tc, alpha, event_times, beta, base_intensity,
         for k in range(len(plan) - BEHIND, len(plan)):
             add_up(k, product_of[k])
 
-        excitation = held.tile([P, BLOCKS], F32, name="excitation")
-        nc.vector.tensor_reduce(
-            excitation[:], partial[:].rearrange("p (b h) -> p b h", h=SLOTS),
-            mybir.AxisListType.X, ALU.add,
-        )
         v = held.tile([P, BLOCKS], F32, name="v")
-        nc.vector.tensor_add(v[:], excitation[:], base[:])
+        nc.vector.tensor_reduce(v[:], parts, mybir.AxisListType.X, ALU.add)
 
         magnitude = held.tile([P, BLOCKS], F32, name="magnitude")
         nc.scalar.activation(magnitude[:], v[:], ACT.Abs)

@@ -11,7 +11,12 @@ SLOTS = len(RAMP)
 PARTS = SLOTS + 1
 AHEAD = 3
 BEHIND = 2
+LAST = BLOCKS - 1
 T_NOW = 4.0
+SQUARES = (-0.93717527, 0.65362424, 4.18560947)
+WEIGHT = -0.0023037299
+CUBIC = (0.82715372, -0.22578705, 0.042602373)
+AT_ZERO = -WEIGHT * ((SQUARES[0] ** 2 + SQUARES[1]) ** 2 + SQUARES[2]) ** 2
 
 F32 = mybir.dt.float32
 U16 = mybir.dt.uint16
@@ -83,17 +88,17 @@ def tile_markedpointprocess_kernel(tc, alpha, event_times, beta, base_intensity,
                 i = (first + place) // P
                 spread(time_columns[:, i : i + 1], slot, place)
 
-        zero = held.tile([P, 1], F32, name="zero")
-        nc.gpsimd.memset(zero[:], 0.0)
-        one = held.tile([P, 1], F32, name="one")
-        nc.scalar.activation(one[:], zero[:], ACT.Exp)
+        shifts = held.tile([P, len(SQUARES)], F32, name="shifts")
+        for i, value in enumerate(SQUARES):
+            nc.gpsimd.memset(shifts[:, i : i + 1], value)
 
         shift = held.tile([P, BLOCKS], F32, name="shift")
         nc.scalar.mul(shift[:], rate[:], -T_NOW)
 
-        partial = held.tile([P, BLOCKS * PARTS], F32, name="partial")
-        parts = partial[:].rearrange("p (b h) -> p b h", h=PARTS)
-        nc.gpsimd.memset(partial[:], 0.0)
+        partial = held.tile([P, BLOCKS * PARTS + RAMP[0]], F32, name="partial")
+        last_products = partial[:, BLOCKS * PARTS :]
+        parts = partial[:, : BLOCKS * PARTS].rearrange("p (b h) -> p b h", h=PARTS)
+        nc.gpsimd.memset(partial[:, : BLOCKS * PARTS], 0.0)
         nc.vector.tensor_copy(parts[:, :, SLOTS : SLOTS + 1], base[:].unsqueeze(2))
 
         def make_decay(k):
@@ -112,19 +117,24 @@ def tile_markedpointprocess_kernel(tc, alpha, event_times, beta, base_intensity,
 
         def look_up_and_multiply(k, decay):
             b, slot, first, width = plan[k]
-            product = products.tile([P, PIECE], F32, name="product")
+            if k == len(plan) - 1:
+                product = last_products
+            else:
+                product = products.tile([P, PIECE], F32, name="product")[:, :width]
             piece = offsets[:, first // 16 : (first + width) // 16]
             nc.vector.tensor_tensor(
-                product[:, :width], windows[b][:].indirect(piece), decay[:, :width], ALU.mult
+                product, windows[b][:].indirect(piece), decay[:, :width], ALU.mult
             )
             return product
 
         def add_up(k, product):
             b, slot, first, width = plan[k]
             nc.scalar.activation(
-                product[:, :width], product[:, :width], ACT.Copy,
+                product, product, ACT.Copy,
                 accum_out=partial[:, b * PARTS + slot : b * PARTS + slot + 1],
             )
+
+        v = held.tile([P, BLOCKS], F32, name="v")
 
         decay_of = {k: make_decay(k) for k in range(AHEAD)}
         product_of = {}
@@ -134,20 +144,32 @@ def tile_markedpointprocess_kernel(tc, alpha, event_times, beta, base_intensity,
                 decay_of[k + AHEAD] = make_decay(k + AHEAD)
             if k >= BEHIND:
                 add_up(k - BEHIND, product_of[k - BEHIND])
-        for k in range(len(plan) - BEHIND, len(plan)):
-            add_up(k, product_of[k])
-
-        v = held.tile([P, BLOCKS], F32, name="v")
-        nc.vector.tensor_reduce(v[:], parts, mybir.AxisListType.X, ALU.add)
+            if k == len(plan) - 3:
+                nc.vector.tensor_reduce(v[:, :LAST], parts[:, :LAST, :], mybir.AxisListType.X, ALU.add)
+        add_up(len(plan) - 2, product_of[len(plan) - 2])
+        nc.vector.tensor_reduce(
+            v[:, LAST:], partial[:, LAST * PARTS :], mybir.AxisListType.X, ALU.add
+        )
 
         magnitude = held.tile([P, BLOCKS], F32, name="magnitude")
         nc.scalar.activation(magnitude[:], v[:], ACT.Abs)
-        small = held.tile([P, BLOCKS], F32, name="small")
-        nc.scalar.activation(small[:], magnitude[:], ACT.Exp, scale=-1.0)
-        log_term = held.tile([P, BLOCKS], F32, name="log_term")
-        nc.scalar.activation(log_term[:], small[:], ACT.Ln, bias=one[:])
+        x = held.tile([P, BLOCKS], F32, name="x")
+        nc.scalar.activation(x[:], magnitude[:], ACT.Exp, scale=-1.0)
+        square = x
+        for i in range(len(SQUARES)):
+            inner = square
+            square = held.tile([P, BLOCKS], F32, name=f"square{i}")
+            nc.scalar.activation(square[:], inner[:], ACT.Square, bias=shifts[:, i : i + 1])
+
         positive = held.tile([P, BLOCKS], F32, name="positive")
-        nc.vector.tensor_scalar_max(positive[:], v[:], 0.0)
+        nc.vector.tensor_scalar(positive[:], v[:], 0.0, AT_ZERO, ALU.max, ALU.add)
+        quadratic = held.tile([P, BLOCKS], F32, name="quadratic")
+        nc.vector.scalar_tensor_tensor(quadratic[:], x[:], CUBIC[1] / CUBIC[2], x[:], ALU.add, ALU.mult)
+        cubic = held.tile([P, BLOCKS], F32, name="cubic")
+        nc.vector.scalar_tensor_tensor(cubic[:], quadratic[:], CUBIC[0] / CUBIC[2], x[:], ALU.add, ALU.mult)
+        rest = held.tile([P, BLOCKS], F32, name="rest")
+        nc.vector.scalar_tensor_tensor(rest[:], cubic[:], CUBIC[2], positive[:], ALU.mult, ALU.add)
+
         result = held.tile([P, BLOCKS], F32, name="result")
-        nc.vector.tensor_add(result[:], positive[:], log_term[:])
+        nc.vector.scalar_tensor_tensor(result[:], square[:], WEIGHT, rest[:], ALU.mult, ALU.add)
         nc.sync.dma_start(out_rows, result[:])

@@ -12,11 +12,12 @@ PARTS = SLOTS + 1
 AHEAD = 3
 BEHIND = 2
 LAST = BLOCKS - 1
+EARLY = BLOCKS - 2
 T_NOW = 4.0
-SQUARES = (-0.93717527, 0.65362424, 4.18560947)
-WEIGHT = -0.0023037299
-CUBIC = (0.82715372, -0.22578705, 0.042602373)
-AT_ZERO = -WEIGHT * ((SQUARES[0] ** 2 + SQUARES[1]) ** 2 + SQUARES[2]) ** 2
+LOG = (0.9999964239, -0.4998741238, 0.3317990258, -0.2407338084,
+       0.1676540711, -0.0953293897, 0.0360884937, -0.0064535442)
+POWERS = len(LOG)
+TERMS = POWERS + 1
 
 F32 = mybir.dt.float32
 U16 = mybir.dt.uint16
@@ -88,9 +89,12 @@ def tile_markedpointprocess_kernel(tc, alpha, event_times, beta, base_intensity,
                 i = (first + place) // P
                 spread(time_columns[:, i : i + 1], slot, place)
 
-        shifts = held.tile([P, len(SQUARES)], F32, name="shifts")
-        for i, value in enumerate(SQUARES):
-            nc.gpsimd.memset(shifts[:, i : i + 1], value)
+        exponents = held.tile([P, POWERS], F32, name="exponents")
+        weights = held.tile([P, TERMS], F32, name="weights")
+        for i, coefficient in enumerate(LOG):
+            nc.vector.memset(exponents[:, i : i + 1], -(i + 1.0))
+            nc.vector.memset(weights[:, i : i + 1], coefficient)
+        nc.vector.memset(weights[:, POWERS:], 1.0)
 
         shift = held.tile([P, BLOCKS], F32, name="shift")
         nc.scalar.mul(shift[:], rate[:], -T_NOW)
@@ -135,6 +139,14 @@ def tile_markedpointprocess_kernel(tc, alpha, event_times, beta, base_intensity,
             )
 
         v = held.tile([P, BLOCKS], F32, name="v")
+        magnitude = held.tile([P, BLOCKS], F32, name="magnitude")
+        terms = held.tile([P, BLOCKS * TERMS], F32, name="terms")
+        terms_of = terms[:].rearrange("p (b i) -> p b i", i=TERMS)
+
+        def make_powers(b):
+            nc.scalar.activation(
+                terms[:, b * TERMS : b * TERMS + POWERS], exponents[:], ACT.Exp, scale=magnitude[:, b : b + 1]
+            )
 
         decay_of = {k: make_decay(k) for k in range(AHEAD)}
         product_of = {}
@@ -144,32 +156,40 @@ def tile_markedpointprocess_kernel(tc, alpha, event_times, beta, base_intensity,
                 decay_of[k + AHEAD] = make_decay(k + AHEAD)
             if k >= BEHIND:
                 add_up(k - BEHIND, product_of[k - BEHIND])
-            if k == len(plan) - 3:
-                nc.vector.tensor_reduce(v[:, :LAST], parts[:, :LAST, :], mybir.AxisListType.X, ALU.add)
+            if k == len(plan) - SLOTS:
+                nc.vector.tensor_reduce(v[:, :EARLY], parts[:, :EARLY, :], mybir.AxisListType.X, ALU.add)
+            if k == len(plan) - SLOTS + 3:
+                nc.scalar.activation(magnitude[:, :EARLY], v[:, :EARLY], ACT.Abs)
+                for b in range(EARLY):
+                    make_powers(b)
+                nc.scalar.activation(
+                    terms_of[:, :EARLY, POWERS:], v[:, :EARLY].unsqueeze(2), ACT.Relu
+                )
         add_up(len(plan) - 2, product_of[len(plan) - 2])
+        nc.vector.tensor_reduce(
+            v[:, EARLY:LAST], parts[:, EARLY:LAST, :], mybir.AxisListType.X, ALU.add
+        )
         nc.vector.tensor_reduce(
             v[:, LAST:], partial[:, LAST * PARTS :], mybir.AxisListType.X, ALU.add
         )
 
-        magnitude = held.tile([P, BLOCKS], F32, name="magnitude")
-        nc.scalar.activation(magnitude[:], v[:], ACT.Abs)
-        x = held.tile([P, BLOCKS], F32, name="x")
-        nc.scalar.activation(x[:], magnitude[:], ACT.Exp, scale=-1.0)
-        square = x
-        for i in range(len(SQUARES)):
-            inner = square
-            square = held.tile([P, BLOCKS], F32, name=f"square{i}")
-            nc.scalar.activation(square[:], inner[:], ACT.Square, bias=shifts[:, i : i + 1])
-
-        positive = held.tile([P, BLOCKS], F32, name="positive")
-        nc.vector.tensor_scalar(positive[:], v[:], 0.0, AT_ZERO, ALU.max, ALU.add)
-        quadratic = held.tile([P, BLOCKS], F32, name="quadratic")
-        nc.vector.scalar_tensor_tensor(quadratic[:], x[:], CUBIC[1] / CUBIC[2], x[:], ALU.add, ALU.mult)
-        cubic = held.tile([P, BLOCKS], F32, name="cubic")
-        nc.vector.scalar_tensor_tensor(cubic[:], quadratic[:], CUBIC[0] / CUBIC[2], x[:], ALU.add, ALU.mult)
-        rest = held.tile([P, BLOCKS], F32, name="rest")
-        nc.vector.scalar_tensor_tensor(rest[:], cubic[:], CUBIC[2], positive[:], ALU.mult, ALU.add)
+        nc.vector.scalar_tensor_tensor(
+            magnitude[:, EARLY:], v[:, EARLY:], -1.0, v[:, EARLY:], ALU.mult, ALU.max
+        )
+        for b in range(EARLY, BLOCKS):
+            make_powers(b)
+        nc.vector.tensor_scalar_max(terms_of[:, EARLY:, POWERS:], v[:, EARLY:].unsqueeze(2), 0.0)
 
         result = held.tile([P, BLOCKS], F32, name="result")
-        nc.vector.scalar_tensor_tensor(result[:], square[:], WEIGHT, rest[:], ALU.mult, ALU.add)
+        weighted = last_products[:, : EARLY * TERMS].rearrange("p (b i) -> p b i", i=TERMS)
+        nc.vector.tensor_tensor(
+            weighted, terms_of[:, :EARLY, :], weights[:].unsqueeze(1).to_broadcast([P, EARLY, TERMS]), ALU.mult
+        )
+        nc.vector.tensor_reduce(result[:, :EARLY], weighted, mybir.AxisListType.X, ALU.add)
+        for b in range(EARLY, BLOCKS):
+            late_weighted = held.tile([P, TERMS], F32, name=f"late_weighted{b}")
+            nc.vector.scalar_tensor_tensor(
+                late_weighted[:], terms[:, b * TERMS : (b + 1) * TERMS], 1.0, weights[:],
+                ALU.mult, ALU.mult, accum_out=result[:, b : b + 1],
+            )
         nc.sync.dma_start(out_rows, result[:])

@@ -6,7 +6,8 @@ C, S, N = 1024, 1024, 2048
 BLOCKS = C // P
 PIECE = S
 BANK = 512
-RAMP = (P, P, 2 * P, BANK, BANK, BANK)
+RAMP = (P, P, P, 2 * P, 3 * P, BANK, BANK)
+ENDING = (BANK, BANK, BANK, 2 * P, P, P)
 SLOTS = len(RAMP)
 PARTS = SLOTS + 1
 AHEAD = 3
@@ -28,7 +29,7 @@ ALU = mybir.AluOpType
 def look_ups():
     widths_of = {b: (PIECE, PIECE) for b in range(BLOCKS)}
     widths_of[0] = RAMP
-    widths_of[BLOCKS - 1] = tuple(reversed(RAMP))
+    widths_of[LAST] = ENDING
     plan = []
     for b in range(BLOCKS):
         first = 0
@@ -99,7 +100,7 @@ def tile_markedpointprocess_kernel(tc, alpha, event_times, beta, base_intensity,
         shift = held.tile([P, BLOCKS], F32, name="shift")
         nc.scalar.mul(shift[:], rate[:], -T_NOW)
 
-        partial = held.tile([P, BLOCKS * PARTS + RAMP[0]], F32, name="partial")
+        partial = held.tile([P, BLOCKS * PARTS + ENDING[-1]], F32, name="partial")
         last_products = partial[:, BLOCKS * PARTS :]
         parts = partial[:, : BLOCKS * PARTS].rearrange("p (b h) -> p b h", h=PARTS)
         nc.gpsimd.memset(partial[:, : BLOCKS * PARTS], 0.0)
@@ -156,9 +157,9 @@ def tile_markedpointprocess_kernel(tc, alpha, event_times, beta, base_intensity,
                 decay_of[k + AHEAD] = make_decay(k + AHEAD)
             if k >= BEHIND:
                 add_up(k - BEHIND, product_of[k - BEHIND])
-            if k == len(plan) - SLOTS:
+            if k == len(plan) - len(ENDING):
                 nc.vector.tensor_reduce(v[:, :EARLY], parts[:, :EARLY, :], mybir.AxisListType.X, ALU.add)
-            if k == len(plan) - SLOTS + 3:
+            if k == len(plan) - len(ENDING) + 3:
                 nc.scalar.activation(magnitude[:, :EARLY], v[:, :EARLY], ACT.Abs)
                 for b in range(EARLY):
                     make_powers(b)

import concourse.mybir as mybir
from concourse.masks import make_identity

P = 128
C, S, N = 1024, 1024, 2048
BLOCKS = C // P
PIECE = S
BANK = 512
RAMP = (P, P, P, 2 * P, 3 * P, BANK, BANK)
ENDING = (BANK, BANK, BANK, 2 * P, P, P)
SLOTS = len(RAMP)
PARTS = SLOTS + 1
AHEAD = 3
BEHIND = 2
LAST = BLOCKS - 1
EARLY = BLOCKS - 2
T_NOW = 4.0
LOG = (0.9999964239, -0.4998741238, 0.3317990258, -0.2407338084,
       0.1676540711, -0.0953293897, 0.0360884937, -0.0064535442)
POWERS = len(LOG)
TERMS = POWERS + 1

F32 = mybir.dt.float32
U16 = mybir.dt.uint16
ACT = mybir.ActivationFunctionType
ALU = mybir.AluOpType


def look_ups():
    widths_of = {b: (PIECE, PIECE) for b in range(BLOCKS)}
    widths_of[0] = RAMP
    widths_of[LAST] = ENDING
    plan = []
    for b in range(BLOCKS):
        first = 0
        for slot, width in enumerate(widths_of[b]):
            plan.append((b, slot, first, width))
            first += width
    return plan


def tile_markedpointprocess_kernel(tc, alpha, event_times, beta, base_intensity, offs, out):
    nc = tc.nc

    alpha_blocks = alpha.rearrange("(p b) s -> b p s", b=BLOCKS)
    beta_rows = beta.rearrange("(p b) o -> p (b o)", b=BLOCKS)
    base_rows = base_intensity.rearrange("(p b) o -> p (b o)", b=BLOCKS)
    out_rows = out.rearrange("(p b) o -> p (b o)", b=BLOCKS)

    with (
        tc.tile_pool(name="held", bufs=1) as held,
        tc.tile_pool(name="decays", bufs=AHEAD + 2) as decays,
        tc.tile_pool(name="products", bufs=BEHIND + SLOTS) as products,
        tc.psum_pool(name="banks", bufs=1) as banks,
    ):
        offsets = held.tile([P, N // 16], U16, name="offsets")
        rate = held.tile([P, BLOCKS], F32, name="rate")
        base = held.tile([P, BLOCKS], F32, name="base")
        time_rows = held.tile([P, P], F32, name="time_rows")
        time_columns = held.tile([P, N // P], F32, name="time_columns")
        first_column = held.tile([P, 1], F32, name="first_column")
        windows = [held.tile([P, S], F32, name=f"window{b}") for b in range(BLOCKS)]

        plan = look_ups()

        nc.gpsimd.memset(time_rows[:], 0.0)
        nc.sync.dma_start(time_rows[: N // P, :], event_times.rearrange("o (i p) -> (o i) p", p=P))
        nc.sync.dma_start(base[:], base_rows)
        nc.scalar.dma_start(first_column[:], event_times[:, :P].rearrange("o p -> p o"))
        nc.scalar.dma_start(rate[:], beta_rows)
        nc.sync.dma_start(offsets[:], offs)
        for b in range(BLOCKS):
            nc.sync.dma_start(windows[b][:], alpha_blocks[b])

        identity = held.tile([P, P], F32, name="identity")
        make_identity(nc, identity[:])
        times = [banks.tile([P, BANK], F32, name=f"times{slot}") for slot in range(SLOTS)]

        def spread(column, slot, place):
            nc.tensor.transpose(
                times[slot][:, place : place + P], column.to_broadcast([P, P]), identity[:]
            )

        spread(first_column[:], 0, 0)
        turned = banks.tile([P, P], F32, name="turned")
        nc.tensor.transpose(turned[:], time_rows[:], identity[:])
        nc.vector.tensor_copy(time_columns[:], turned[:, : N // P])
        for b, slot, first, width in plan[1:SLOTS]:
            for place in range(0, width, P):
                i = (first + place) // P
                spread(time_columns[:, i : i + 1], slot, place)

        exponents = held.tile([P, POWERS], F32, name="exponents")
        weights = held.tile([P, TERMS], F32, name="weights")
        for i, coefficient in enumerate(LOG):
            nc.vector.memset(exponents[:, i : i + 1], -(i + 1.0))
            nc.vector.memset(weights[:, i : i + 1], coefficient)
        nc.vector.memset(weights[:, POWERS:], 1.0)

        shift = held.tile([P, BLOCKS], F32, name="shift")
        nc.scalar.mul(shift[:], rate[:], -T_NOW)

        partial = held.tile([P, BLOCKS * PARTS + ENDING[-1]], F32, name="partial")
        last_products = partial[:, BLOCKS * PARTS :]
        parts = partial[:, : BLOCKS * PARTS].rearrange("p (b h) -> p b h", h=PARTS)
        nc.gpsimd.memset(partial[:, : BLOCKS * PARTS], 0.0)
        nc.vector.tensor_copy(parts[:, :, SLOTS : SLOTS + 1], base[:].unsqueeze(2))

        def make_decay(k):
            b, slot, first, width = plan[k]
            decay = decays.tile([P, PIECE], F32, name="decay")
            for block0, bank, bank_first, bank_width in plan[:SLOTS]:
                lo = max(first, bank_first)
                hi = min(first + width, bank_first + bank_width)
                if lo < hi:
                    nc.scalar.activation(
                        decay[:, lo - first : hi - first],
                        times[bank][:, lo - bank_first : hi - bank_first], ACT.Exp,
                        bias=shift[:, b : b + 1], scale=rate[:, b : b + 1],
                    )
            return decay

        def look_up_and_multiply(k, decay):
            b, slot, first, width = plan[k]
            if k == len(plan) - 1:
                product = last_products
            else:
                product = products.tile([P, PIECE], F32, name="product")[:, :width]
            piece = offsets[:, first // 16 : (first + width) // 16]
            nc.vector.tensor_tensor(
                product, windows[b][:].indirect(piece), decay[:, :width], ALU.mult
            )
            return product

        def add_up(k, product):
            b, slot, first, width = plan[k]
            nc.scalar.activation(
                product, product, ACT.Copy,
                accum_out=partial[:, b * PARTS + slot : b * PARTS + slot + 1],
            )

        v = held.tile([P, BLOCKS], F32, name="v")
        magnitude = held.tile([P, BLOCKS], F32, name="magnitude")
        terms = held.tile([P, BLOCKS * TERMS], F32, name="terms")
        terms_of = terms[:].rearrange("p (b i) -> p b i", i=TERMS)

        def make_powers(b):
            nc.scalar.activation(
                terms[:, b * TERMS : b * TERMS + POWERS], exponents[:], ACT.Exp, scale=magnitude[:, b : b + 1]
            )

        decay_of = {k: make_decay(k) for k in range(AHEAD)}
        product_of = {}
        for k in range(len(plan)):
            product_of[k] = look_up_and_multiply(k, decay_of[k])
            if k + AHEAD < len(plan):
                decay_of[k + AHEAD] = make_decay(k + AHEAD)
            if k >= BEHIND:
                add_up(k - BEHIND, product_of[k - BEHIND])
            if k == len(plan) - len(ENDING):
                nc.vector.tensor_reduce(v[:, :EARLY], parts[:, :EARLY, :], mybir.AxisListType.X, ALU.add)
            if k == len(plan) - len(ENDING) + 3:
                nc.scalar.activation(magnitude[:, :EARLY], v[:, :EARLY], ACT.Abs)
                for b in range(EARLY):
                    make_powers(b)
                nc.scalar.activation(
                    terms_of[:, :EARLY, POWERS:], v[:, :EARLY].unsqueeze(2), ACT.Relu
                )
        add_up(len(plan) - 2, product_of[len(plan) - 2])
        nc.vector.tensor_reduce(
            v[:, EARLY:LAST], parts[:, EARLY:LAST, :], mybir.AxisListType.X, ALU.add
        )
        nc.vector.tensor_reduce(
            v[:, LAST:], partial[:, LAST * PARTS :], mybir.AxisListType.X, ALU.add
        )

        nc.vector.scalar_tensor_tensor(
            magnitude[:, EARLY:], v[:, EARLY:], -1.0, v[:, EARLY:], ALU.mult, ALU.max
        )
        for b in range(EARLY, BLOCKS):
            make_powers(b)
        nc.vector.tensor_scalar_max(terms_of[:, EARLY:, POWERS:], v[:, EARLY:].unsqueeze(2), 0.0)

        result = held.tile([P, BLOCKS], F32, name="result")
        weighted = last_products[:, : EARLY * TERMS].rearrange("p (b i) -> p b i", i=TERMS)
        nc.vector.tensor_tensor(
            weighted, terms_of[:, :EARLY, :], weights[:].unsqueeze(1).to_broadcast([P, EARLY, TERMS]), ALU.mult
        )
        nc.vector.tensor_reduce(result[:, :EARLY], weighted, mybir.AxisListType.X, ALU.add)
        for b in range(EARLY, BLOCKS):
            late_weighted = held.tile([P, TERMS], F32, name=f"late_weighted{b}")
            nc.vector.scalar_tensor_tensor(
                late_weighted[:], terms[:, b * TERMS : (b + 1) * TERMS], 1.0, weights[:],
                ALU.mult, ALU.mult, accum_out=result[:, b : b + 1],
            )
        nc.sync.dma_start(out_rows, result[:])
